import numpy as np
import ml_dtypes


def mxq(x, axis, fmt="e4m3"):
    dtype, down = {"e4m3": (ml_dtypes.float8_e4m3fn, 7), "e5m2": (ml_dtypes.float8_e5m2, 14)}[fmt]
    v = np.moveaxis(np.asarray(x, np.float32).astype(ml_dtypes.bfloat16).astype(np.float64), axis, -1)
    blocks = v.reshape(v.shape[:-1] + (-1, 32))
    amax = np.abs(blocks).max(-1, keepdims=True)
    byte = np.maximum(np.where(amax > 0, np.frexp(amax)[1] - 1 + 127, 0) - down, 1)
    scale = np.exp2(byte - 127.0)
    codes = (blocks / scale).astype(np.float32).astype(dtype).astype(np.float64)
    return np.moveaxis((codes * scale).reshape(v.shape), -1, axis)


WIDE = False


def mx_kscale(k):
    if not WIDE:
        return np.ones(k)
    levels = np.array([10, -10, 5, -5, 0])
    if k % 512:
        return np.exp2(np.random.permutation(np.resize(levels, k // 32))).repeat(32)
    a = np.empty((k // 512, 16))
    for p in range(k // 512):
        a[p, :8] = np.random.permutation(np.resize(levels, 8))
        for g in range(8):
            far = levels[np.abs(levels - a[p, g]) >= 10]
            a[p, g + 8] = far[np.random.randint(len(far))]
    return np.exp2(a.ravel()).repeat(32)


BF16 = ml_dtypes.bfloat16


def bf(x):
    return np.asarray(x, np.float32).astype(BF16)


def f64(x):
    return np.asarray(x).astype(np.float64)


B, N, D, F, M1, M2 = 4, 128, 512, 2048, 3, 5
D2 = D + D


def silu(v):
    return v / (1.0 + np.exp(-v))


def draw0():
    s, t = mx_kscale(D), mx_kscale(D2)
    return {"h": bf(np.random.standard_normal((B, N, D)) * t[:D]),
            "x1": bf(np.random.standard_normal((B, N, D, M1)) * s[:, None]),
            "pre1": bf(np.random.standard_normal((D, D)) / np.sqrt(D) / s[:, None] * t[D:]),
            "w1_0": bf(np.random.standard_normal((D2, F)) / np.sqrt(D2) / t[:, None]),
            "b1_0": bf(np.random.standard_normal(F) * 0.2)}


def core(h, x1, pre1, w1_0, b1_0):
    xt = f64(x1).swapaxes(-1, -2).reshape(B * N * M1, D)
    pm = (mxq(xt, 1, "e4m3") @ mxq(f64(pre1), 0, "e4m3")).reshape(B, N, M1, D)
    inv = np.sqrt(np.sum(pm * pm, axis=-2))
    mlp_in = np.concatenate([f64(h), inv], axis=-1)
    return silu((mxq(mlp_in, 2, "e4m3") @ mxq(f64(w1_0), 0, "e4m3")) + f64(b1_0))


def e4m3fn_bytes(y):
    return np.clip(np.asarray(y, np.float64), -448.0, 448.0).astype(np.float32).astype(ml_dtypes.float8_e4m3fn).view(np.uint8)


def e4m3fn_values(b):
    return np.asarray(b, np.uint8).view(ml_dtypes.float8_e4m3fn).astype(np.float64)


def setup_inputs():
    d = draw0()
    x0 = np.asarray(d['w1_0']).astype(np.float64)
    s = (np.max(np.abs(x0), axis=(1,), keepdims=True) / 448.0).astype(np.float32)
    out = {}
    for k, v in d.items():
        if k == 'w1_0':
            out['w1_0_bytes'] = e4m3fn_bytes(x0 / s.astype(np.float64))
            out['w1_0_scale'] = s
        else:
            out[k] = v
    return out


def reference(h, x1, pre1, w1_0_bytes, w1_0_scale, b1_0):
    return core(h, x1, pre1, e4m3fn_values(w1_0_bytes) * w1_0_scale.astype(np.float64), b1_0)

@@ -1,0 +1,251 @@
+from contextlib import ExitStack
+
+import concourse.mybir as mybir
+from concourse.masks import make_identity
+
+F32 = mybir.dt.float32
+BF16 = mybir.dt.bfloat16
+U8 = mybir.dt.uint8
+U32 = mybir.dt.uint32
+FP8 = mybir.dt.float8_e4m3fn
+FP8X4 = mybir.dt.float8_e4m3fn_x4
+ACT = mybir.ActivationFunctionType
+ALU = mybir.AluOpType
+
+P = 128
+TOK = 512
+D = 512
+M1 = 3
+FF = 2048
+NT = TOK // P
+FQ = 512
+NQ = FF // FQ
+
+FLOPS = 2 * TOK * M1 * D * D + 2 * TOK * 2 * D * FF
+
+
+ORDER = """
+x.1.2.0 x.1.1.1 w.0.0.1.1 x.1.0.1 x.3.0.1 x.3.1.1 w.0.2.0.0 x.2.0.1 x.2.1.1 w.1.3.1.1 w.0.0.0.0 x.0.1.1
+w.0.2.1.0 pi w.1.0.1.0 x.0.0.1 w.1.0.0.0 x.0.2.1 xq.1.0 pq w.0.3.0.0 xq.1.1 w.1.3.0.0 xq.0.1
+w.0.1.0.0 xq.0.0 iv.0.0 x.2.2.1 mm.1.3 mm.0.3 w.1.2.0.0 mm.0.2 mm.0.0 mm.1.0 wq.0.0 x.3.2.0
+w.0.1.1.0 xq.1.2 w.1.1.1.0 xq.0.2 mm.1.2 it.0.1 mm.1.1 mm.0.1 w.1.1.0.0 h.1.1 ad.1.1 mm.2.2
+hq.1 ad.1.0 it.1.0 mm.2.3 mm.2.1 w.0.3.1.1 iv.1.1 mm.2.0 wq.1.0 w.1.2.1.1 ad.2.1 ad.2.0
+wq.1.1 h.0.1 iv.1.2 rt.1 aq.1 wq.0.1 wq.1.2 it.0.2 rt.0 b.3.0 b.2.0 hq.0
+aq.0 f.3.0 b.2.1 b.3.1 f.2.0 f.3.1 f.2.1 iv.0.3 b.1.0 wq.0.2 b.0.0 it.1.3
+f.1.0 b.0.1 b.0.2 b.1.2 b.1.1 f.0.0 f.0.1 wq.0.3 f.0.2 wq.1.3 f.1.2 b.2.2
+b.1.3 b.2.3 b.0.3 f.1.1 f.2.2 f.1.3 b.3.3 f.2.3 f.0.3 b.3.2 f.3.3 f.3.2
+"""
+
+
+def tile_equivariantfeedforward_pa_kernel(tc, h, x1, pre1, w1_0_bytes, w1_0_scale, b1_0, out):
+    nc = tc.nc
+    with ExitStack() as ctx:
+        keep = ctx.enter_context(tc.tile_pool(name="keep", bufs=1))
+        work = ctx.enter_context(tc.tile_pool(name="work", bufs=3))
+        outs = ctx.enter_context(tc.tile_pool(name="outs", bufs=6))
+        psum_tr = ctx.enter_context(tc.psum_pool(name="psum_tr", bufs=3))
+        psum_mm = ctx.enter_context(tc.psum_pool(name="psum_mm", bufs=5))
+
+        w_view = w1_0_bytes.rearrange("(g p t) n -> g t p n", p=P, t=4)
+        wb = {}
+        for g in range(2):
+            for t in range(4):
+                wb[g, t] = keep.tile([P, FF], U8, name=f"wb{g}{t}", align_bytes=64)
+        xs = [keep.tile([P, D * M1], BF16, name=f"xs{i}", align_bytes=64) for i in range(NT)]
+        hs = keep.tile([P, NT, D], BF16, name="hs", align_bytes=64)
+        pre_raw = keep.tile([P, 4, D], BF16, name="pre_raw", align_bytes=64)
+        ws = keep.tile([P, 2, 4], F32, name="ws", align_bytes=64)
+        bias = keep.tile([P, FF], BF16, name="bias", align_bytes=64)
+
+        def load_w(g, t):
+            nc.sync.dma_start(out=wb[g, t][:], in_=w_view[g][t])
+
+        def load_x(i):
+            nc.sync.dma_start(out=xs[i][:], in_=x1[i].rearrange("n d m -> n (d m)"))
+
+        nc.scalar.dma_start(out=ws[:], in_=w1_0_scale.rearrange("(g p t) o -> p g (t o)", p=P, t=4))
+        load_x(1)
+        load_w(0, 0)
+        load_w(0, 2)
+        load_x(3)
+        nc.sync.dma_start(out=pre_raw[:], in_=pre1.rearrange("(p j) e -> p j e", j=4))
+        load_x(2)
+        load_w(1, 0)
+        load_x(0)
+        load_w(1, 3)
+        load_w(0, 3)
+        load_w(0, 1)
+        nc.sync.dma_start(out=hs[:], in_=h.rearrange("b n d -> n b d"))
+        load_w(1, 2)
+        nc.sync.dma_start(out=bias[:], in_=b1_0.partition_broadcast(P))
+        load_w(1, 1)
+
+        ident_bf = keep.tile([P, P], BF16, name="ident_bf", align_bytes=64)
+        make_identity(nc, ident_bf[:])
+        ident_f = keep.tile([P, P], F32, name="ident_f", align_bytes=64)
+        make_identity(nc, ident_f[:])
+
+        warm = keep.tile([P, 1], F32, name="warm")
+        nc.vector.memset(warm[:], 1.0)
+        nc.scalar.activation(out=warm[:], in_=warm[:], func=ACT.Sqrt)
+
+        planes = [keep.tile([P, 4, FF], BF16, name=f"planes{g}", align_bytes=64) for g in range(2)]
+        w_codes = [keep.tile([P, FF], U32, name=f"w_codes{g}", align_bytes=64) for g in range(2)]
+        w_scales = [keep.tile([P, FF], U8, name=f"w_scales{g}", align_bytes=64) for g in range(2)]
+        x_int = [keep.tile([P, TOK, 4], BF16, name=f"x_int{m}", align_bytes=64) for m in range(M1)]
+        x_codes = [keep.tile([P, TOK], U32, name=f"x_codes{m}", align_bytes=64) for m in range(M1)]
+        x_scales = [keep.tile([P, TOK], U8, name=f"x_scales{m}", align_bytes=64) for m in range(M1)]
+        pre_int = keep.tile([P, 4 * P, 4], BF16, name="pre_int", align_bytes=64)
+        pre_codes = keep.tile([P, D], U32, name="pre_codes", align_bytes=64)
+        pre_scales = keep.tile([P, D], U8, name="pre_scales", align_bytes=64)
+        a_int = [keep.tile([P, TOK, 4], BF16, name=f"a_int{g}", align_bytes=64) for g in range(2)]
+        a_codes = [keep.tile([P, TOK], U32, name=f"a_codes{g}", align_bytes=64) for g in range(2)]
+        a_scales = [keep.tile([P, TOK], U8, name=f"a_scales{g}", align_bytes=64) for g in range(2)]
+        sq = [keep.tile([P, 4, TOK], F32, name=f"sq{m}", align_bytes=64) for m in range(M1)]
+
+        def widen_v(g, t, c0, c1):
+            nc.vector.tensor_scalar(
+                out=planes[g][:, t, c0:c1], in0=wb[g, t][:, c0:c1].bitcast(FP8),
+                scalar1=ws[:, g, t : t + 1], scalar2=None, op0=ALU.mult)
+
+        def widen_s(g, t, c0, c1):
+            nc.scalar.activation(
+                out=planes[g][:, t, c0:c1], in_=wb[g, t][:, c0:c1].bitcast(FP8),
+                func=ACT.Copy, scale=ws[:, g, t : t + 1])
+
+        def inter_w(g, q):
+            w_int = work.tile([P, FQ, 4], BF16, name="w_int", align_bytes=64)
+            src = planes[g][:, :, q * FQ : (q + 1) * FQ]
+            nc.vector.tensor_copy(out=w_int[:], in_=src.rearrange("p t n -> p n t"))
+            return w_int
+
+        def inter_w_tensor(g, q):
+            w_int = work.tile([P, FQ, 4], BF16, name="w_int", align_bytes=64)
+            for k in range(2):
+                tr = psum_tr.tile([P, 2, P, 4], BF16, name="tr")
+                for j in range(2):
+                    c0 = q * FQ + (2 * k + j) * P
+                    nc.tensor.matmul(tr[:, j, :, :].rearrange("p n t -> p (n t)"), lhsT=ident_bf[:],
+                                     rhs=planes[g][:, :, c0 : c0 + P].rearrange("p t n -> p n t"), start=True, stop=True)
+                nc.scalar.copy(out=w_int[:, 2 * k * P : 2 * (k + 1) * P, :].rearrange("p n t -> p (n t)"),
+                               in_=tr[:].rearrange("p j n t -> p (j n t)"))
+            return w_int
+
+        def quant_w(g, q, w_int):
+            c = slice(q * FQ, (q + 1) * FQ)
+            nc.vector.quantize_mx(out=w_codes[g][:, c].bitcast(FP8X4), scales=w_scales[g][:, c],
+                                  in_=w_int[:].rearrange("p n t -> p (n t)"))
+
+        def x_tile(i, m, on_scalar):
+            tr = psum_tr.tile([P, 4, P], BF16, name="tr")
+            for t in range(4):
+                nc.tensor.transpose(tr[:, t, :], xs[i][:, 3 * t + m : D * M1 : 12], ident_bf[:])
+            copy = nc.scalar.copy if on_scalar else nc.vector.tensor_copy
+            copy(out=x_int[m][:, i * P : (i + 1) * P, :], in_=tr[:].rearrange("p t n -> p n t"))
+
+        def x_quant(half, m):
+            c = slice(half * 256, half * 256 + 256)
+            nc.vector.quantize_mx(out=x_codes[m][:, c].bitcast(FP8X4), scales=x_scales[m][:, c],
+                                  in_=x_int[m][:, c, :].rearrange("p n t -> p (n t)"))
+
+        def pre_inter():
+            nc.vector.tensor_copy(out=pre_int[:].rearrange("p (t m) j -> p t m j", t=4),
+                                  in_=pre_raw[:].rearrange("p j (m t) -> p t m j", t=4))
+
+        def pre_quant():
+            nc.vector.quantize_mx(out=pre_codes[:].bitcast(FP8X4), scales=pre_scales[:],
+                                  in_=pre_int[:].rearrange("p n j -> p (n j)"))
+
+        def h_tiles(k, on_scalar):
+            i0 = 2 * k
+            words = hs[:].rearrange("p i d -> p (i d)").bitcast(F32)
+            tr = psum_tr.tile([P, 2, 2, P], F32, name="tr")
+            for i in range(2):
+                w0 = (i0 + i) * (D // 2)
+                for u in range(2):
+                    nc.tensor.transpose(tr[:, i, u, :], words[:, w0 + u : w0 + D // 2 : 2], ident_f[:])
+            dst = a_int[0][:].rearrange("p n t -> p (n t)").bitcast(F32)
+            dst = dst[:, i0 * 256 : (i0 + 2) * 256].rearrange("p (i n u) -> p i n u", i=2, u=2)
+            copy = nc.scalar.copy if on_scalar else nc.vector.tensor_copy
+            copy(out=dst, in_=tr[:].rearrange("p i u n -> p i n u"))
+
+        def quant_a(g, half):
+            c = slice(half * 256, half * 256 + 256)
+            nc.vector.quantize_mx(out=a_codes[g][:, c].bitcast(FP8X4), scales=a_scales[g][:, c],
+                                  in_=a_int[g][:, c, :].rearrange("p n t -> p (n t)"))
+
+        def mm1(m, t):
+            acc = psum_mm.tile([P, TOK], F32, name="acc")
+            c = slice(t * P, (t + 1) * P)
+            nc.tensor.matmul_mx(out=acc[:], lhsT=pre_codes[:, c].bitcast(FP8X4), lhsT_scale=pre_scales[:, c],
+                                rhs=x_codes[m][:].bitcast(FP8X4), rhs_scale=x_scales[m][:], start=True, stop=True)
+            nc.scalar.activation(out=sq[m][:, t, :], in_=acc[:], func=ACT.Square)
+
+        def add(m, t0):
+            nc.vector.tensor_tensor(out=sq[0][:, t0 : t0 + 2, :], in0=sq[0][:, t0 : t0 + 2, :],
+                                    in1=sq[m][:, t0 : t0 + 2, :], op=ALU.add)
+
+        def root(half):
+            c = slice(half * 256, half * 256 + 256)
+            nc.scalar.activation(out=a_int[1][:, c, :], in_=sq[0][:, :, c].rearrange("p t n -> p n t"), func=ACT.Sqrt)
+
+        def mm2(i, q):
+            acc = psum_mm.tile([P, FQ], F32, name="acc")
+            r = slice(i * P, (i + 1) * P)
+            c = slice(q * FQ, (q + 1) * FQ)
+            for g in range(2):
+                nc.tensor.matmul_mx(out=acc[:], lhsT=a_codes[g][:, r].bitcast(FP8X4), lhsT_scale=a_scales[g][:, r],
+                                    rhs=w_codes[g][:, c].bitcast(FP8X4), rhs_scale=w_scales[g][:, c],
+                                    start=(g == 0), stop=(g == 1))
+            o = outs.tile([P, FQ], F32, name="o", align_bytes=64)
+            nc.vector.tensor_tensor(out=o[:], in0=acc[:], in1=bias[:, c], op=ALU.add)
+            return o
+
+        def finish(i, q, o):
+            nc.scalar.activation(out=o[:], in_=o[:], func=ACT.Silu)
+            nc.sync.dma_start(out=out[i][:, q * FQ : (q + 1) * FQ], in_=o[:])
+
+        w_int = {}
+        o = {}
+
+        def widen(g, t, half, on_scalar):
+            (widen_s if on_scalar else widen_v)(g, t, half * 1024, half * 1024 + 1024)
+
+        def step(kind, a):
+            if kind == "w":
+                widen(a[0], a[1], a[2], a[3])
+            elif kind == "x":
+                x_tile(a[0], a[1], a[2])
+            elif kind == "xq":
+                x_quant(a[0], a[1])
+            elif kind == "pi":
+                pre_inter()
+            elif kind == "pq":
+                pre_quant()
+            elif kind == "h":
+                h_tiles(a[0], a[1])
+            elif kind == "hq":
+                quant_a(0, a[0])
+            elif kind == "mm":
+                mm1(a[0], a[1])
+            elif kind == "ad":
+                add(a[0], 2 * a[1])
+            elif kind == "rt":
+                root(a[0])
+            elif kind == "aq":
+                quant_a(1, a[0])
+            elif kind == "iv":
+                w_int[a[0], a[1]] = inter_w(a[0], a[1])
+            elif kind == "it":
+                w_int[a[0], a[1]] = inter_w_tensor(a[0], a[1])
+            elif kind == "wq":
+                quant_w(a[0], a[1], w_int[a[0], a[1]])
+            elif kind == "b":
+                o[a[0], a[1]] = mm2(a[0], a[1])
+            elif kind == "f":
+                finish(a[0], a[1], o[a[0], a[1]])
+
+        with tc.manual_schedule():
+            for word in ORDER.split():
+                parts = word.split(".")
+                step(parts[0], [int(v) for v in parts[1:]])

@@ -25,15 +25,15 @@ FLOPS = 2 * TOK * M1 * D * D + 2 * TOK * 2 * D * FF
 
 
 ORDER = """
-x.1.2.0 x.1.1.1 w.0.0.1.1 x.1.0.1 x.3.0.1 x.3.1.1 w.0.2.0.0 x.2.0.1 x.2.1.1 w.1.3.1.1 w.0.0.0.0 x.0.1.1
-w.0.2.1.0 pi w.1.0.1.0 x.0.0.1 w.1.0.0.0 x.0.2.1 xq.1.0 pq w.0.3.0.0 xq.1.1 w.1.3.0.0 xq.0.1
-w.0.1.0.0 xq.0.0 iv.0.0 x.2.2.1 mm.1.3 mm.0.3 w.1.2.0.0 mm.0.2 mm.0.0 mm.1.0 wq.0.0 x.3.2.0
-w.0.1.1.0 xq.1.2 w.1.1.1.0 xq.0.2 mm.1.2 it.0.1 mm.1.1 mm.0.1 w.1.1.0.0 h.1.1 ad.1.1 mm.2.2
-hq.1 ad.1.0 it.1.0 mm.2.3 mm.2.1 w.0.3.1.1 iv.1.1 mm.2.0 wq.1.0 w.1.2.1.1 ad.2.1 ad.2.0
-wq.1.1 h.0.1 iv.1.2 rt.1 aq.1 wq.0.1 wq.1.2 it.0.2 rt.0 b.3.0 b.2.0 hq.0
-aq.0 f.3.0 b.2.1 b.3.1 f.2.0 f.3.1 f.2.1 iv.0.3 b.1.0 wq.0.2 b.0.0 it.1.3
-f.1.0 b.0.1 b.0.2 b.1.2 b.1.1 f.0.0 f.0.1 wq.0.3 f.0.2 wq.1.3 f.1.2 b.2.2
-b.1.3 b.2.3 b.0.3 f.1.1 f.2.2 f.1.3 b.3.3 f.2.3 f.0.3 b.3.2 f.3.3 f.3.2
+w.0.2.0.1 x.0.1.1 w.0.2.1.0 w.1.0.1.1 w.0.0.0.0 w.1.0.0.0 x.0.0.1 w.0.0.1.0 w.0.3.1.0 w.0.3.0.0 x.0.2.1 w.1.2.0.0
+x.3.0.1 x.3.1.1 x.2.1.0 w.1.2.1.1 w.0.1.1.1 x.2.0.0 x.1.0.1 w.0.1.0.1 xq.1.1 x.1.2.1 xq.1.0 pi
+x.1.1.1 xq.0.0 h.0.1 pq mm.0.0 iv.0.0.0 xq.0.1 mm.0.2 x.3.2.1 xq.0.2 mm.1.3 wq.0.0
+x.2.2.1 w.1.1.0.0 mm.1.2 iv.0.1.0 mm.0.1 xq.1.2 mm.0.3 mm.1.0 wq.0.1 w.1.1.1.0 mm.2.0 mm.1.1
+mm.2.2 ad.1.1 w.1.3.0.0 ad.1.0 mm.2.3 mm.2.1 ad.2.1 ad.2.0 h.1.1 iv.1.0.1 rt.0 iv.1.1.0
+hq.0 wq.1.0 wq.1.1 w.1.3.1.0 iv.0.3.0 aq.0 wq.0.3 rt.1 iv.1.3.0 hq.1 aq.1 iv.0.2.1
+b.1.0 iv.1.2.1 b.0.1 f.1.0 b.3.0 b.1.1 b.3.1 b.2.1 f.1.1 f.0.1 wq.1.3 b.2.0
+f.3.1 wq.0.2 wq.1.2 b.0.0 b.3.3 f.2.1 f.2.0 f.3.0 b.0.2 b.0.3 f.0.0 f.3.3
+b.1.2 f.0.2 b.3.2 f.0.3 b.1.3 f.1.2 f.3.2 b.2.2 f.1.3 b.2.3 f.2.2 f.2.3
 """
 
 
@@ -42,7 +42,7 @@ def tile_equivariantfeedforward_pa_kernel(tc, h, x1, pre1, w1_0_bytes, w1_0_scal
     with ExitStack() as ctx:
         keep = ctx.enter_context(tc.tile_pool(name="keep", bufs=1))
         work = ctx.enter_context(tc.tile_pool(name="work", bufs=3))
-        outs = ctx.enter_context(tc.tile_pool(name="outs", bufs=6))
+        outs = ctx.enter_context(tc.tile_pool(name="outs", bufs=12))
         psum_tr = ctx.enter_context(tc.psum_pool(name="psum_tr", bufs=3))
         psum_mm = ctx.enter_context(tc.psum_pool(name="psum_mm", bufs=5))
 
@@ -64,21 +64,21 @@ def tile_equivariantfeedforward_pa_kernel(tc, h, x1, pre1, w1_0_bytes, w1_0_scal
             nc.sync.dma_start(out=xs[i][:], in_=x1[i].rearrange("n d m -> n (d m)"))
 
         nc.scalar.dma_start(out=ws[:], in_=w1_0_scale.rearrange("(g p t) o -> p g (t o)", p=P, t=4))
-        load_x(1)
-        load_w(0, 0)
         load_w(0, 2)
-        load_x(3)
-        nc.sync.dma_start(out=pre_raw[:], in_=pre1.rearrange("(p j) e -> p j e", j=4))
-        load_x(2)
-        load_w(1, 0)
         load_x(0)
-        load_w(1, 3)
+        load_w(0, 0)
+        load_w(1, 0)
+        load_x(3)
         load_w(0, 3)
-        load_w(0, 1)
-        nc.sync.dma_start(out=hs[:], in_=h.rearrange("b n d -> n b d"))
+        load_x(2)
         load_w(1, 2)
-        nc.sync.dma_start(out=bias[:], in_=b1_0.partition_broadcast(P))
+        load_w(0, 1)
+        load_x(1)
+        nc.sync.dma_start(out=pre_raw[:], in_=pre1.rearrange("(p j) e -> p j e", j=4))
+        nc.sync.dma_start(out=hs[:], in_=h.rearrange("b n d -> n b d"))
         load_w(1, 1)
+        load_w(1, 3)
+        nc.sync.dma_start(out=bias[:], in_=b1_0.partition_broadcast(P))
 
         ident_bf = keep.tile([P, P], BF16, name="ident_bf", align_bytes=64)
         make_identity(nc, ident_bf[:])
@@ -113,10 +113,18 @@ def tile_equivariantfeedforward_pa_kernel(tc, h, x1, pre1, w1_0_bytes, w1_0_scal
                 out=planes[g][:, t, c0:c1], in_=wb[g, t][:, c0:c1].bitcast(FP8),
                 func=ACT.Copy, scale=ws[:, g, t : t + 1])
 
-        def inter_w(g, q):
+        def inter_w(g, q, engine):
             w_int = work.tile([P, FQ, 4], BF16, name="w_int", align_bytes=64)
-            src = planes[g][:, :, q * FQ : (q + 1) * FQ]
-            nc.vector.tensor_copy(out=w_int[:], in_=src.rearrange("p t n -> p n t"))
+            src = planes[g][:, :, q * FQ : (q + 1) * FQ].rearrange("p t n -> p n t")
+            if engine == 2:
+                for k in range(2):
+                    c = slice(k * 256, k * 256 + 256)
+                    nc.gpsimd.tensor_scalar(out=w_int[:, c, :], in0=src[:, c, :], scalar1=1.0, scalar2=0.0,
+                                            op0=ALU.mult, op1=ALU.add)
+            elif engine == 1:
+                nc.scalar.copy(out=w_int[:], in_=src)
+            else:
+                nc.vector.tensor_copy(out=w_int[:], in_=src)
             return w_int
 
         def inter_w_tensor(g, q):
@@ -235,7 +243,7 @@ def tile_equivariantfeedforward_pa_kernel(tc, h, x1, pre1, w1_0_bytes, w1_0_scal
             elif kind == "aq":
                 quant_a(1, a[0])
             elif kind == "iv":
-                w_int[a[0], a[1]] = inter_w(a[0], a[1])
+                w_int[a[0], a[1]] = inter_w(a[0], a[1], a[2])
             elif kind == "it":
                 w_int[a[0], a[1]] = inter_w_tensor(a[0], a[1])
             elif kind == "wq":

@@ -25,15 +25,15 @@ FLOPS = 2 * TOK * M1 * D * D + 2 * TOK * 2 * D * FF
 
 
 ORDER = """
-w.0.2.0.1 x.0.1.1 w.0.2.1.0 w.1.0.1.1 w.0.0.0.0 w.1.0.0.0 x.0.0.1 w.0.0.1.0 w.0.3.1.0 w.0.3.0.0 x.0.2.1 w.1.2.0.0
-x.3.0.1 x.3.1.1 x.2.1.0 w.1.2.1.1 w.0.1.1.1 x.2.0.0 x.1.0.1 w.0.1.0.1 xq.1.1 x.1.2.1 xq.1.0 pi
-x.1.1.1 xq.0.0 h.0.1 pq mm.0.0 iv.0.0.0 xq.0.1 mm.0.2 x.3.2.1 xq.0.2 mm.1.3 wq.0.0
-x.2.2.1 w.1.1.0.0 mm.1.2 iv.0.1.0 mm.0.1 xq.1.2 mm.0.3 mm.1.0 wq.0.1 w.1.1.1.0 mm.2.0 mm.1.1
-mm.2.2 ad.1.1 w.1.3.0.0 ad.1.0 mm.2.3 mm.2.1 ad.2.1 ad.2.0 h.1.1 iv.1.0.1 rt.0 iv.1.1.0
-hq.0 wq.1.0 wq.1.1 w.1.3.1.0 iv.0.3.0 aq.0 wq.0.3 rt.1 iv.1.3.0 hq.1 aq.1 iv.0.2.1
-b.1.0 iv.1.2.1 b.0.1 f.1.0 b.3.0 b.1.1 b.3.1 b.2.1 f.1.1 f.0.1 wq.1.3 b.2.0
-f.3.1 wq.0.2 wq.1.2 b.0.0 b.3.3 f.2.1 f.2.0 f.3.0 b.0.2 b.0.3 f.0.0 f.3.3
-b.1.2 f.0.2 b.3.2 f.0.3 b.1.3 f.1.2 f.3.2 b.2.2 f.1.3 b.2.3 f.2.2 f.2.3
+dx.0.1 dx.1.0 pi.1 x.0.0.0 dx.3.1 dx.2.0 x.0.1.1 pq w.0.2.1.0 x.0.2.1 xq.0.0 w.0.0.1.0
+w.1.1.1.0 xq.0.1 w.1.0.1.1 x.1.2.1 x.1.0.1 w.1.1.0.0 xq.0.2 xq.1.0 x.1.1.1 xq.1.1 w.0.1.0.0 w.0.3.0.1
+w.1.0.0.1 mm.0.1 w.0.0.0.0 w.1.3.0.0 mm.1.3 xq.1.2 mm.0.3 w.1.2.0.0 mm.1.2 mm.0.2 mm.2.2 w.0.3.1.0
+mm.1.0 w.0.2.0.0 w.1.3.1.0 mm.0.0 ad.1.1.0 mm.2.1 h.0.0 mm.1.1 mm.2.3 iv.1.0.0 it.0.1 mm.2.0
+ad.1.0.1 ad.2.1.1 ad.2.0.0 w.1.2.1.1 wq.0.1 wq.1.0 it.0.0 rt.0 iv.1.1.0 w.0.1.1.0 it.1.2 wq.1.1
+aq.0 wq.0.0 h.1.1 hq.0 wq.1.2 hq.1 rt.1 aq.1 b.0.1 iv.0.2.1 b.1.0 iv.1.3.0
+b.1.1 b.3.0 f.0.1 wq.0.2 it.0.3 wq.1.3 b.3.1 f.3.0 b.0.2 f.1.1 b.2.1 b.0.0
+f.1.0 f.0.2 wq.0.3 f.3.1 b.2.2 f.2.1 b.2.0 b.0.3 f.0.0 b.3.2 f.2.2 f.2.0
+f.0.3 b.2.3 b.1.2 f.3.2 f.2.3 b.1.3 b.3.3 f.1.2 f.1.3 f.3.3
 """
 
 
@@ -64,21 +64,21 @@ def tile_equivariantfeedforward_pa_kernel(tc, h, x1, pre1, w1_0_bytes, w1_0_scal
             nc.sync.dma_start(out=xs[i][:], in_=x1[i].rearrange("n d m -> n (d m)"))
 
         nc.scalar.dma_start(out=ws[:], in_=w1_0_scale.rearrange("(g p t) o -> p g (t o)", p=P, t=4))
-        load_w(0, 2)
         load_x(0)
-        load_w(0, 0)
-        load_w(1, 0)
-        load_x(3)
-        load_w(0, 3)
-        load_x(2)
-        load_w(1, 2)
-        load_w(0, 1)
         load_x(1)
         nc.sync.dma_start(out=pre_raw[:], in_=pre1.rearrange("(p j) e -> p j e", j=4))
-        nc.sync.dma_start(out=hs[:], in_=h.rearrange("b n d -> n b d"))
+        load_x(3)
+        load_x(2)
+        load_w(1, 0)
+        load_w(0, 2)
+        load_w(0, 0)
         load_w(1, 1)
+        load_w(1, 2)
+        load_w(0, 3)
+        load_w(0, 1)
         load_w(1, 3)
         nc.sync.dma_start(out=bias[:], in_=b1_0.partition_broadcast(P))
+        nc.sync.dma_start(out=hs[:], in_=h.rearrange("b n d -> n b d"))
 
         ident_bf = keep.tile([P, P], BF16, name="ident_bf", align_bytes=64)
         make_identity(nc, ident_bf[:])
@@ -92,6 +92,7 @@ def tile_equivariantfeedforward_pa_kernel(tc, h, x1, pre1, w1_0_bytes, w1_0_scal
         planes = [keep.tile([P, 4, FF], BF16, name=f"planes{g}", align_bytes=64) for g in range(2)]
         w_codes = [keep.tile([P, FF], U32, name=f"w_codes{g}", align_bytes=64) for g in range(2)]
         w_scales = [keep.tile([P, FF], U8, name=f"w_scales{g}", align_bytes=64) for g in range(2)]
+        x_m = [keep.tile([P, M1, D], BF16, name=f"x_m{i}", align_bytes=64) for i in range(NT)]
         x_int = [keep.tile([P, TOK, 4], BF16, name=f"x_int{m}", align_bytes=64) for m in range(M1)]
         x_codes = [keep.tile([P, TOK], U32, name=f"x_codes{m}", align_bytes=64) for m in range(M1)]
         x_scales = [keep.tile([P, TOK], U8, name=f"x_scales{m}", align_bytes=64) for m in range(M1)]
@@ -144,21 +145,44 @@ def tile_equivariantfeedforward_pa_kernel(tc, h, x1, pre1, w1_0_bytes, w1_0_scal
             nc.vector.quantize_mx(out=w_codes[g][:, c].bitcast(FP8X4), scales=w_scales[g][:, c],
                                   in_=w_int[:].rearrange("p n t -> p (n t)"))
 
-        def x_tile(i, m, on_scalar):
-            tr = psum_tr.tile([P, 4, P], BF16, name="tr")
-            for t in range(4):
-                nc.tensor.transpose(tr[:, t, :], xs[i][:, 3 * t + m : D * M1 : 12], ident_bf[:])
+        def split_x(i, engine):
+            src = xs[i][:].rearrange("p (d m) -> p m d", m=M1)
+            if engine == 2:
+                for k in range(2):
+                    c = slice(k * 256, k * 256 + 256)
+                    nc.gpsimd.tensor_scalar(out=x_m[i][:, :, c], in0=src[:, :, c], scalar1=1.0, scalar2=0.0,
+                                            op0=ALU.mult, op1=ALU.add)
+            elif engine == 1:
+                nc.scalar.copy(out=x_m[i][:], in_=src)
+            else:
+                nc.vector.tensor_copy(out=x_m[i][:], in_=src)
+
+        def x_tiles(half, m, on_scalar):
+            tr = psum_tr.tile([P, 2, 2, P], F32, name="tr")
+            for i in range(2):
+                words = x_m[2 * half + i][:].rearrange("p m d -> p (m d)").bitcast(F32)
+                for u in range(2):
+                    w0 = m * (D // 2)
+                    nc.tensor.transpose(tr[:, i, u, :], words[:, w0 + u : w0 + D // 2 : 2], ident_f[:])
+            dst = x_int[m][:].rearrange("p n t -> p (n t)").bitcast(F32)
+            dst = dst[:, half * 512 : (half + 1) * 512].rearrange("p (i n u) -> p i n u", i=2, u=2)
             copy = nc.scalar.copy if on_scalar else nc.vector.tensor_copy
-            copy(out=x_int[m][:, i * P : (i + 1) * P, :], in_=tr[:].rearrange("p t n -> p n t"))
+            copy(out=dst, in_=tr[:].rearrange("p i u n -> p i n u"))
 
         def x_quant(half, m):
             c = slice(half * 256, half * 256 + 256)
             nc.vector.quantize_mx(out=x_codes[m][:, c].bitcast(FP8X4), scales=x_scales[m][:, c],
                                   in_=x_int[m][:, c, :].rearrange("p n t -> p (n t)"))
 
-        def pre_inter():
-            nc.vector.tensor_copy(out=pre_int[:].rearrange("p (t m) j -> p t m j", t=4),
-                                  in_=pre_raw[:].rearrange("p j (m t) -> p t m j", t=4))
+        def pre_inter(engine):
+            dst = pre_int[:].rearrange("p (t m) j -> p t m j", t=4)
+            src = pre_raw[:].rearrange("p j (m t) -> p t m j", t=4)
+            if engine == 2:
+                for t in range(4):
+                    nc.gpsimd.tensor_scalar(out=dst[:, t], in0=src[:, t], scalar1=1.0, scalar2=0.0,
+                                            op0=ALU.mult, op1=ALU.add)
+            else:
+                nc.vector.tensor_copy(out=dst, in_=src)
 
         def pre_quant():
             nc.vector.quantize_mx(out=pre_codes[:].bitcast(FP8X4), scales=pre_scales[:],
@@ -189,9 +213,13 @@ def tile_equivariantfeedforward_pa_kernel(tc, h, x1, pre1, w1_0_bytes, w1_0_scal
                                 rhs=x_codes[m][:].bitcast(FP8X4), rhs_scale=x_scales[m][:], start=True, stop=True)
             nc.scalar.activation(out=sq[m][:, t, :], in_=acc[:], func=ACT.Square)
 
-        def add(m, t0):
-            nc.vector.tensor_tensor(out=sq[0][:, t0 : t0 + 2, :], in0=sq[0][:, t0 : t0 + 2, :],
-                                    in1=sq[m][:, t0 : t0 + 2, :], op=ALU.add)
+        def add(m, t0, engine):
+            if engine == 2:
+                for t in (t0, t0 + 1):
+                    nc.gpsimd.tensor_tensor(out=sq[0][:, t, :], in0=sq[0][:, t, :], in1=sq[m][:, t, :], op=ALU.add)
+            else:
+                nc.vector.tensor_tensor(out=sq[0][:, t0 : t0 + 2, :], in0=sq[0][:, t0 : t0 + 2, :],
+                                        in1=sq[m][:, t0 : t0 + 2, :], op=ALU.add)
 
         def root(half):
             c = slice(half * 256, half * 256 + 256)
@@ -223,11 +251,13 @@ def tile_equivariantfeedforward_pa_kernel(tc, h, x1, pre1, w1_0_bytes, w1_0_scal
             if kind == "w":
                 widen(a[0], a[1], a[2], a[3])
             elif kind == "x":
-                x_tile(a[0], a[1], a[2])
+                x_tiles(a[0], a[1], a[2])
+            elif kind == "dx":
+                split_x(a[0], a[1])
             elif kind == "xq":
                 x_quant(a[0], a[1])
             elif kind == "pi":
-                pre_inter()
+                pre_inter(a[0])
             elif kind == "pq":
                 pre_quant()
             elif kind == "h":
@@ -237,7 +267,7 @@ def tile_equivariantfeedforward_pa_kernel(tc, h, x1, pre1, w1_0_bytes, w1_0_scal
             elif kind == "mm":
                 mm1(a[0], a[1])
             elif kind == "ad":
-                add(a[0], 2 * a[1])
+                add(a[0], 2 * a[1], a[2])
             elif kind == "rt":
                 root(a[0])
             elif kind == "aq":

from contextlib import ExitStack

import concourse.mybir as mybir
from concourse.masks import make_identity

F32 = mybir.dt.float32
BF16 = mybir.dt.bfloat16
U8 = mybir.dt.uint8
U32 = mybir.dt.uint32
FP8 = mybir.dt.float8_e4m3fn
FP8X4 = mybir.dt.float8_e4m3fn_x4
ACT = mybir.ActivationFunctionType
ALU = mybir.AluOpType

P = 128
TOK = 512
D = 512
M1 = 3
FF = 2048
NT = TOK // P
FQ = 512
NQ = FF // FQ

FLOPS = 2 * TOK * M1 * D * D + 2 * TOK * 2 * D * FF


ORDER = """
dx.0.1 dx.1.0 pi.1 x.0.0.0 dx.3.1 dx.2.0 x.0.1.1 pq w.0.2.1.0 x.0.2.1 xq.0.0 w.0.0.1.0
w.1.1.1.0 xq.0.1 w.1.0.1.1 x.1.2.1 x.1.0.1 w.1.1.0.0 xq.0.2 xq.1.0 x.1.1.1 xq.1.1 w.0.1.0.0 w.0.3.0.1
w.1.0.0.1 mm.0.1 w.0.0.0.0 w.1.3.0.0 mm.1.3 xq.1.2 mm.0.3 w.1.2.0.0 mm.1.2 mm.0.2 mm.2.2 w.0.3.1.0
mm.1.0 w.0.2.0.0 w.1.3.1.0 mm.0.0 ad.1.1.0 mm.2.1 h.0.0 mm.1.1 mm.2.3 iv.1.0.0 it.0.1 mm.2.0
ad.1.0.1 ad.2.1.1 ad.2.0.0 w.1.2.1.1 wq.0.1 wq.1.0 it.0.0 rt.0 iv.1.1.0 w.0.1.1.0 it.1.2 wq.1.1
aq.0 wq.0.0 h.1.1 hq.0 wq.1.2 hq.1 rt.1 aq.1 b.0.1 iv.0.2.1 b.1.0 iv.1.3.0
b.1.1 b.3.0 f.0.1 wq.0.2 it.0.3 wq.1.3 b.3.1 f.3.0 b.0.2 f.1.1 b.2.1 b.0.0
f.1.0 f.0.2 wq.0.3 f.3.1 b.2.2 f.2.1 b.2.0 b.0.3 f.0.0 b.3.2 f.2.2 f.2.0
f.0.3 b.2.3 b.1.2 f.3.2 f.2.3 b.1.3 b.3.3 f.1.2 f.1.3 f.3.3
"""


def tile_equivariantfeedforward_pa_kernel(tc, h, x1, pre1, w1_0_bytes, w1_0_scale, b1_0, out):
    nc = tc.nc
    with ExitStack() as ctx:
        keep = ctx.enter_context(tc.tile_pool(name="keep", bufs=1))
        work = ctx.enter_context(tc.tile_pool(name="work", bufs=3))
        outs = ctx.enter_context(tc.tile_pool(name="outs", bufs=12))
        psum_tr = ctx.enter_context(tc.psum_pool(name="psum_tr", bufs=3))
        psum_mm = ctx.enter_context(tc.psum_pool(name="psum_mm", bufs=5))

        w_view = w1_0_bytes.rearrange("(g p t) n -> g t p n", p=P, t=4)
        wb = {}
        for g in range(2):
            for t in range(4):
                wb[g, t] = keep.tile([P, FF], U8, name=f"wb{g}{t}", align_bytes=64)
        xs = [keep.tile([P, D * M1], BF16, name=f"xs{i}", align_bytes=64) for i in range(NT)]
        hs = keep.tile([P, NT, D], BF16, name="hs", align_bytes=64)
        pre_raw = keep.tile([P, 4, D], BF16, name="pre_raw", align_bytes=64)
        ws = keep.tile([P, 2, 4], F32, name="ws", align_bytes=64)
        bias = keep.tile([P, FF], BF16, name="bias", align_bytes=64)

        def load_w(g, t):
            nc.sync.dma_start(out=wb[g, t][:], in_=w_view[g][t])

        def load_x(i):
            nc.sync.dma_start(out=xs[i][:], in_=x1[i].rearrange("n d m -> n (d m)"))

        nc.scalar.dma_start(out=ws[:], in_=w1_0_scale.rearrange("(g p t) o -> p g (t o)", p=P, t=4))
        load_x(0)
        load_x(1)
        nc.sync.dma_start(out=pre_raw[:], in_=pre1.rearrange("(p j) e -> p j e", j=4))
        load_x(3)
        load_x(2)
        load_w(1, 0)
        load_w(0, 2)
        load_w(0, 0)
        load_w(1, 1)
        load_w(1, 2)
        load_w(0, 3)
        load_w(0, 1)
        load_w(1, 3)
        nc.sync.dma_start(out=bias[:], in_=b1_0.partition_broadcast(P))
        nc.sync.dma_start(out=hs[:], in_=h.rearrange("b n d -> n b d"))

        ident_bf = keep.tile([P, P], BF16, name="ident_bf", align_bytes=64)
        make_identity(nc, ident_bf[:])
        ident_f = keep.tile([P, P], F32, name="ident_f", align_bytes=64)
        make_identity(nc, ident_f[:])

        warm = keep.tile([P, 1], F32, name="warm")
        nc.vector.memset(warm[:], 1.0)
        nc.scalar.activation(out=warm[:], in_=warm[:], func=ACT.Sqrt)

        planes = [keep.tile([P, 4, FF], BF16, name=f"planes{g}", align_bytes=64) for g in range(2)]
        w_codes = [keep.tile([P, FF], U32, name=f"w_codes{g}", align_bytes=64) for g in range(2)]
        w_scales = [keep.tile([P, FF], U8, name=f"w_scales{g}", align_bytes=64) for g in range(2)]
        x_m = [keep.tile([P, M1, D], BF16, name=f"x_m{i}", align_bytes=64) for i in range(NT)]
        x_int = [keep.tile([P, TOK, 4], BF16, name=f"x_int{m}", align_bytes=64) for m in range(M1)]
        x_codes = [keep.tile([P, TOK], U32, name=f"x_codes{m}", align_bytes=64) for m in range(M1)]
        x_scales = [keep.tile([P, TOK], U8, name=f"x_scales{m}", align_bytes=64) for m in range(M1)]
        pre_int = keep.tile([P, 4 * P, 4], BF16, name="pre_int", align_bytes=64)
        pre_codes = keep.tile([P, D], U32, name="pre_codes", align_bytes=64)
        pre_scales = keep.tile([P, D], U8, name="pre_scales", align_bytes=64)
        a_int = [keep.tile([P, TOK, 4], BF16, name=f"a_int{g}", align_bytes=64) for g in range(2)]
        a_codes = [keep.tile([P, TOK], U32, name=f"a_codes{g}", align_bytes=64) for g in range(2)]
        a_scales = [keep.tile([P, TOK], U8, name=f"a_scales{g}", align_bytes=64) for g in range(2)]
        sq = [keep.tile([P, 4, TOK], F32, name=f"sq{m}", align_bytes=64) for m in range(M1)]

        def widen_v(g, t, c0, c1):
            nc.vector.tensor_scalar(
                out=planes[g][:, t, c0:c1], in0=wb[g, t][:, c0:c1].bitcast(FP8),
                scalar1=ws[:, g, t : t + 1], scalar2=None, op0=ALU.mult)

        def widen_s(g, t, c0, c1):
            nc.scalar.activation(
                out=planes[g][:, t, c0:c1], in_=wb[g, t][:, c0:c1].bitcast(FP8),
                func=ACT.Copy, scale=ws[:, g, t : t + 1])

        def inter_w(g, q, engine):
            w_int = work.tile([P, FQ, 4], BF16, name="w_int", align_bytes=64)
            src = planes[g][:, :, q * FQ : (q + 1) * FQ].rearrange("p t n -> p n t")
            if engine == 2:
                for k in range(2):
                    c = slice(k * 256, k * 256 + 256)
                    nc.gpsimd.tensor_scalar(out=w_int[:, c, :], in0=src[:, c, :], scalar1=1.0, scalar2=0.0,
                                            op0=ALU.mult, op1=ALU.add)
            elif engine == 1:
                nc.scalar.copy(out=w_int[:], in_=src)
            else:
                nc.vector.tensor_copy(out=w_int[:], in_=src)
            return w_int

        def inter_w_tensor(g, q):
            w_int = work.tile([P, FQ, 4], BF16, name="w_int", align_bytes=64)
            for k in range(2):
                tr = psum_tr.tile([P, 2, P, 4], BF16, name="tr")
                for j in range(2):
                    c0 = q * FQ + (2 * k + j) * P
                    nc.tensor.matmul(tr[:, j, :, :].rearrange("p n t -> p (n t)"), lhsT=ident_bf[:],
                                     rhs=planes[g][:, :, c0 : c0 + P].rearrange("p t n -> p n t"), start=True, stop=True)
                nc.scalar.copy(out=w_int[:, 2 * k * P : 2 * (k + 1) * P, :].rearrange("p n t -> p (n t)"),
                               in_=tr[:].rearrange("p j n t -> p (j n t)"))
            return w_int

        def quant_w(g, q, w_int):
            c = slice(q * FQ, (q + 1) * FQ)
            nc.vector.quantize_mx(out=w_codes[g][:, c].bitcast(FP8X4), scales=w_scales[g][:, c],
                                  in_=w_int[:].rearrange("p n t -> p (n t)"))

        def split_x(i, engine):
            src = xs[i][:].rearrange("p (d m) -> p m d", m=M1)
            if engine == 2:
                for k in range(2):
                    c = slice(k * 256, k * 256 + 256)
                    nc.gpsimd.tensor_scalar(out=x_m[i][:, :, c], in0=src[:, :, c], scalar1=1.0, scalar2=0.0,
                                            op0=ALU.mult, op1=ALU.add)
            elif engine == 1:
                nc.scalar.copy(out=x_m[i][:], in_=src)
            else:
                nc.vector.tensor_copy(out=x_m[i][:], in_=src)

        def x_tiles(half, m, on_scalar):
            tr = psum_tr.tile([P, 2, 2, P], F32, name="tr")
            for i in range(2):
                words = x_m[2 * half + i][:].rearrange("p m d -> p (m d)").bitcast(F32)
                for u in range(2):
                    w0 = m * (D // 2)
                    nc.tensor.transpose(tr[:, i, u, :], words[:, w0 + u : w0 + D // 2 : 2], ident_f[:])
            dst = x_int[m][:].rearrange("p n t -> p (n t)").bitcast(F32)
            dst = dst[:, half * 512 : (half + 1) * 512].rearrange("p (i n u) -> p i n u", i=2, u=2)
            copy = nc.scalar.copy if on_scalar else nc.vector.tensor_copy
            copy(out=dst, in_=tr[:].rearrange("p i u n -> p i n u"))

        def x_quant(half, m):
            c = slice(half * 256, half * 256 + 256)
            nc.vector.quantize_mx(out=x_codes[m][:, c].bitcast(FP8X4), scales=x_scales[m][:, c],
                                  in_=x_int[m][:, c, :].rearrange("p n t -> p (n t)"))

        def pre_inter(engine):
            dst = pre_int[:].rearrange("p (t m) j -> p t m j", t=4)
            src = pre_raw[:].rearrange("p j (m t) -> p t m j", t=4)
            if engine == 2:
                for t in range(4):
                    nc.gpsimd.tensor_scalar(out=dst[:, t], in0=src[:, t], scalar1=1.0, scalar2=0.0,
                                            op0=ALU.mult, op1=ALU.add)
            else:
                nc.vector.tensor_copy(out=dst, in_=src)

        def pre_quant():
            nc.vector.quantize_mx(out=pre_codes[:].bitcast(FP8X4), scales=pre_scales[:],
                                  in_=pre_int[:].rearrange("p n j -> p (n j)"))

        def h_tiles(k, on_scalar):
            i0 = 2 * k
            words = hs[:].rearrange("p i d -> p (i d)").bitcast(F32)
            tr = psum_tr.tile([P, 2, 2, P], F32, name="tr")
            for i in range(2):
                w0 = (i0 + i) * (D // 2)
                for u in range(2):
                    nc.tensor.transpose(tr[:, i, u, :], words[:, w0 + u : w0 + D // 2 : 2], ident_f[:])
            dst = a_int[0][:].rearrange("p n t -> p (n t)").bitcast(F32)
            dst = dst[:, i0 * 256 : (i0 + 2) * 256].rearrange("p (i n u) -> p i n u", i=2, u=2)
            copy = nc.scalar.copy if on_scalar else nc.vector.tensor_copy
            copy(out=dst, in_=tr[:].rearrange("p i u n -> p i n u"))

        def quant_a(g, half):
            c = slice(half * 256, half * 256 + 256)
            nc.vector.quantize_mx(out=a_codes[g][:, c].bitcast(FP8X4), scales=a_scales[g][:, c],
                                  in_=a_int[g][:, c, :].rearrange("p n t -> p (n t)"))

        def mm1(m, t):
            acc = psum_mm.tile([P, TOK], F32, name="acc")
            c = slice(t * P, (t + 1) * P)
            nc.tensor.matmul_mx(out=acc[:], lhsT=pre_codes[:, c].bitcast(FP8X4), lhsT_scale=pre_scales[:, c],
                                rhs=x_codes[m][:].bitcast(FP8X4), rhs_scale=x_scales[m][:], start=True, stop=True)
            nc.scalar.activation(out=sq[m][:, t, :], in_=acc[:], func=ACT.Square)

        def add(m, t0, engine):
            if engine == 2:
                for t in (t0, t0 + 1):
                    nc.gpsimd.tensor_tensor(out=sq[0][:, t, :], in0=sq[0][:, t, :], in1=sq[m][:, t, :], op=ALU.add)
            else:
                nc.vector.tensor_tensor(out=sq[0][:, t0 : t0 + 2, :], in0=sq[0][:, t0 : t0 + 2, :],
                                        in1=sq[m][:, t0 : t0 + 2, :], op=ALU.add)

        def root(half):
            c = slice(half * 256, half * 256 + 256)
            nc.scalar.activation(out=a_int[1][:, c, :], in_=sq[0][:, :, c].rearrange("p t n -> p n t"), func=ACT.Sqrt)

        def mm2(i, q):
            acc = psum_mm.tile([P, FQ], F32, name="acc")
            r = slice(i * P, (i + 1) * P)
            c = slice(q * FQ, (q + 1) * FQ)
            for g in range(2):
                nc.tensor.matmul_mx(out=acc[:], lhsT=a_codes[g][:, r].bitcast(FP8X4), lhsT_scale=a_scales[g][:, r],
                                    rhs=w_codes[g][:, c].bitcast(FP8X4), rhs_scale=w_scales[g][:, c],
                                    start=(g == 0), stop=(g == 1))
            o = outs.tile([P, FQ], F32, name="o", align_bytes=64)
            nc.vector.tensor_tensor(out=o[:], in0=acc[:], in1=bias[:, c], op=ALU.add)
            return o

        def finish(i, q, o):
            nc.scalar.activation(out=o[:], in_=o[:], func=ACT.Silu)
            nc.sync.dma_start(out=out[i][:, q * FQ : (q + 1) * FQ], in_=o[:])

        w_int = {}
        o = {}

        def widen(g, t, half, on_scalar):
            (widen_s if on_scalar else widen_v)(g, t, half * 1024, half * 1024 + 1024)

        def step(kind, a):
            if kind == "w":
                widen(a[0], a[1], a[2], a[3])
            elif kind == "x":
                x_tiles(a[0], a[1], a[2])
            elif kind == "dx":
                split_x(a[0], a[1])
            elif kind == "xq":
                x_quant(a[0], a[1])
            elif kind == "pi":
                pre_inter(a[0])
            elif kind == "pq":
                pre_quant()
            elif kind == "h":
                h_tiles(a[0], a[1])
            elif kind == "hq":
                quant_a(0, a[0])
            elif kind == "mm":
                mm1(a[0], a[1])
            elif kind == "ad":
                add(a[0], 2 * a[1], a[2])
            elif kind == "rt":
                root(a[0])
            elif kind == "aq":
                quant_a(1, a[0])
            elif kind == "iv":
                w_int[a[0], a[1]] = inter_w(a[0], a[1], a[2])
            elif kind == "it":
                w_int[a[0], a[1]] = inter_w_tensor(a[0], a[1])
            elif kind == "wq":
                quant_w(a[0], a[1], w_int[a[0], a[1]])
            elif kind == "b":
                o[a[0], a[1]] = mm2(a[0], a[1])
            elif kind == "f":
                finish(a[0], a[1], o[a[0], a[1]])

        with tc.manual_schedule():
            for word in ORDER.split():
                parts = word.split(".")
                step(parts[0], [int(v) for v in parts[1:]])
